import numpy as np
import ml_dtypes


def mxq(x, axis, fmt="e4m3"):
    dtype, down = {"e4m3": (ml_dtypes.float8_e4m3fn, 7), "e5m2": (ml_dtypes.float8_e5m2, 14)}[fmt]
    v = np.moveaxis(np.asarray(x, np.float32).astype(ml_dtypes.bfloat16).astype(np.float64), axis, -1)
    blocks = v.reshape(v.shape[:-1] + (-1, 32))
    amax = np.abs(blocks).max(-1, keepdims=True)
    byte = np.maximum(np.where(amax > 0, np.frexp(amax)[1] - 1 + 127, 0) - down, 1)
    scale = np.exp2(byte - 127.0)
    codes = (blocks / scale).astype(np.float32).astype(dtype).astype(np.float64)
    return np.moveaxis((codes * scale).reshape(v.shape), -1, axis)


WIDE = False


def mx_kscale(k):
    if not WIDE:
        return np.ones(k)
    levels = np.array([10, -10, 5, -5, 0])
    if k % 512:
        return np.exp2(np.random.permutation(np.resize(levels, k // 32))).repeat(32)
    a = np.empty((k // 512, 16))
    for p in range(k // 512):
        a[p, :8] = np.random.permutation(np.resize(levels, 8))
        for g in range(8):
            far = levels[np.abs(levels - a[p, g]) >= 10]
            a[p, g + 8] = far[np.random.randint(len(far))]
    return np.exp2(a.ravel()).repeat(32)


BF16 = ml_dtypes.bfloat16


def bf(x):
    return np.asarray(x, np.float32).astype(BF16)


def f64(x):
    return np.asarray(x).astype(np.float64)


B, A, E, P, R = 1024, 8, 1024, 512, 256


def setup_inputs():
    s_src, s_edge = mx_kscale(E), mx_kscale(E)
    t = mx_kscale(P)
    s_cat = np.concatenate([s_src, s_edge])
    return {
        "image_features": bf(np.random.standard_normal((B, E)) * s_src),
        "edge_attributes": bf(np.random.standard_normal((B, A, E)) * s_edge),
        "linear_w": bf(np.random.standard_normal((P, 2 * E)) / np.sqrt(2 * E) / s_cat * t[:, None]),
        "linear_b": bf(np.random.standard_normal(P) * 0.3 * t),
        "fwd_proj": bf(np.random.standard_normal((A, P, R)) / np.sqrt(P) / t[:, None]),
    }


def reference(image_features, edge_attributes, linear_w, linear_b, fwd_proj):
    w = f64(linear_w)
    node = mxq(f64(image_features), 1, "e4m3") @ mxq(w[:, :E].T, 0, "e4m3")
    edge = (mxq(f64(edge_attributes).reshape(B * A, E), 1, "e4m3") @ mxq(w[:, E:].T, 0, "e4m3")).reshape(B, A, P)
    agg = node[:, None, :] + edge + f64(linear_b)
    rep = mxq(agg.transpose(1, 0, 2), 2, "e4m3") @ mxq(f64(fwd_proj), 1, "e4m3")
    return rep.transpose(1, 0, 2)

@@ -1,0 +1,248 @@
+from contextlib import ExitStack
+
+import concourse.bass as bass
+import concourse.mybir as mybir
+import concourse.tile as tile
+from concourse.masks import make_identity
+
+F32 = mybir.dt.float32
+BF16 = mybir.dt.bfloat16
+U32 = mybir.dt.uint32
+U8 = mybir.dt.uint8
+FP8X4 = mybir.dt.float8_e4m3fn_x4
+ADD = mybir.AluOpType.add
+
+B, A, E, P, R = 1024, 8, 1024, 512, 256
+FLOPS = 2 * (B * E * P + B * A * E * P + B * A * P * R)
+
+MANUAL = True
+XBUFS = 6
+REGROUP = {2: (("s", 0), ("s", 1)), 3: (("s", 2), ("s", 3)), 4: (("s", 4), ("s", 5)), 5: (("s", 6), ("s", 7))}
+QF = {4: 0, 6: 1}
+RSTART = 7
+RSLOTS = (0, 1, 2)
+LATE_SLOTS = (1, 2, 3)
+
+
+def tile_attributegnn_pa_t_kernel(tc, image_features, edge_attributes, linear_w, linear_b, fwd_proj, out):
+    nc = tc.nc
+    w_v = linear_w.rearrange("(q t) (h k) -> h q t k", t=4, h=2)
+    img_v = image_features.rearrange("(c j) k -> c (j k)", j=8)
+    ea_v = edge_attributes.rearrange("(c j) a k -> c j (a k)", j=8)
+    f_v = fwd_proj.rearrange("a (q t) r -> q a (t r)", t=4)
+    out_v = out.rearrange("(c j) a r -> c j (a r)", j=8)
+    b_v = linear_b.rearrange("(q t) -> q t", t=4)
+
+    with ExitStack() as ctx:
+        const = ctx.enter_context(tc.tile_pool(name="const", bufs=1))
+        xpool = ctx.enter_context(tc.tile_pool(name="xpool", bufs=XBUFS))
+        gpool = ctx.enter_context(tc.tile_pool(name="gpool", bufs=3))
+        cpool = ctx.enter_context(tc.tile_pool(name="cpool", bufs=3))
+        apool = ctx.enter_context(tc.tile_pool(name="apool", bufs=3))
+        rpool = ctx.enter_context(tc.tile_pool(name="rpool", bufs=16))
+        opool = ctx.enter_context(tc.tile_pool(name="opool", bufs=3))
+        psum = ctx.enter_context(tc.psum_pool(name="psum", bufs=1))
+        if MANUAL:
+            ctx.enter_context(tc.manual_schedule())
+
+        banks_used = [0]
+
+        def next_bank():
+            k = banks_used[0] % 8
+            banks_used[0] += 1
+            return psum.tile([128, 512], F32, name="bank%d" % k, tag="bank%d" % k)
+
+        ident = const.tile([128, 128], F32, name="ident")
+        make_identity(nc, ident[:])
+        bias_bf = const.tile([128, 4], BF16, name="bias_bf")
+        with nc.allow_non_contiguous_dma(reason="512 bias values, four to a partition"):
+            nc.scalar.dma_start(out=bias_bf[:], in_=b_v)
+        bias32 = const.tile([128, 4], F32, name="bias32")
+        nc.vector.tensor_copy(out=bias32[:], in_=bias_bf[:])
+        nodeb = const.tile([128, 4096], F32, name="nodeb")
+        w_codes = [const.tile([128, 1024], U32, name="w_codes%d" % h, align_bytes=64) for h in range(2)]
+        w_scales = [const.tile([128, 1024], U8, name="w_scales%d" % h, align_bytes=64) for h in range(2)]
+        f_codes = const.tile([128, 2048], U32, name="f_codes", align_bytes=64)
+        f_scales = const.tile([128, 2048], U8, name="f_scales", align_bytes=64)
+        f_raw = [const.tile([128, 4096], BF16, name="f_raw%d" % h) for h in range(2)]
+        f_grp = [const.tile([128, 4096], BF16, name="f_grp%d" % h, align_bytes=64) for h in range(2)]
+
+        jobs = [("node", 0, 0)] + [("edge", u // 2, u % 2) for u in range(8)]
+        jobs = jobs + [("node", 1, 0)] + [("edge", u // 2, u % 2) for u in range(8, 16)]
+        njobs = len(jobs)
+
+        srcs = [("w", 0), ("job", 0), ("w", 1)] + [("job", i) for i in range(1, njobs)]
+        x_tiles = []
+
+        def load_next():
+            n = len(x_tiles)
+            if n >= len(srcs):
+                return
+            kind, idx = srcs[n]
+            x = xpool.tile([128, 4096], BF16, name="x", tag="x")
+            if kind == "w":
+                for t in range(4):
+                    nc.sync.dma_start(out=x[:, t * 1024:(t + 1) * 1024], in_=w_v[idx][:, t, :])
+            else:
+                jk, j0, j1 = jobs[idx]
+                if jk == "node" and n < 3:
+                    for t in range(4):
+                        c0 = j0 * 4096 + t * 1024
+                        nc.sync.dma_start(out=x[:, t * 1024:(t + 1) * 1024], in_=img_v[:, c0:c0 + 1024])
+                elif jk == "node":
+                    nc.sync.dma_start(out=x[:], in_=img_v[:, j0 * 4096:(j0 + 1) * 4096])
+                else:
+                    nc.sync.dma_start(out=x[:], in_=ea_v[:, j0, j1 * 4096:(j1 + 1) * 4096])
+            x_tiles.append(x)
+            if n == 4 or n == 5:
+                h = n - 4
+                nc.sync.dma_start(out=f_raw[h][:].rearrange("p (a s) -> p a s", a=4), in_=f_v[:, h * 4:(h + 1) * 4, :])
+
+        def transpose_unit(n):
+            x32 = x_tiles[n][:].bitcast(F32)
+            g = gpool.tile([128, 4096], BF16, name="g", tag="g", align_bytes=64)
+            g32 = g[:].bitcast(F32).rearrange("p (r g a c u) -> p r g a c u", r=2, g=2, a=2, c=128, u=2)
+            for aa in range(4):
+                xt = next_bank()
+                for s in range(4):
+                    col = aa * 512 + (s // 2) * 256 + s % 2
+                    nc.tensor.transpose(xt[:, s * 128:(s + 1) * 128], x32[:, col:col + 255:2], ident[:])
+                nc.scalar.copy(out=g32[:, aa // 2, :, aa % 2, :, :],
+                               in_=xt[:].rearrange("p (g u c) -> p g c u", g=2, u=2, c=128))
+            load_next()
+            return g
+
+        def quantise_half(g, codes, scales, r):
+            nc.vector.quantize_mx(out=codes[:, r * 512:(r + 1) * 512].bitcast(FP8X4),
+                                  scales=scales[:, r * 512:(r + 1) * 512],
+                                  in_=g[:, r * 2048:(r + 1) * 2048])
+
+        def project(h, codes, scales, aa):
+            acc = next_bank()
+            for t in range(4):
+                for gi in range(2):
+                    wc = (t // 2) * 512 + gi * 256 + (t % 2) * 128
+                    dc = (aa // 2) * 512 + gi * 256 + (aa % 2) * 128
+                    nc.tensor.matmul_mx(out=acc[:, t * 128:(t + 1) * 128],
+                                        lhsT=w_codes[h][:, wc:wc + 128].bitcast(FP8X4),
+                                        lhsT_scale=w_scales[h][:, wc:wc + 128],
+                                        rhs=codes[:, dc:dc + 128].bitcast(FP8X4),
+                                        rhs_scale=scales[:, dc:dc + 128],
+                                        start=(gi == 0), stop=(gi == 1))
+            return acc
+
+        pending = []
+        done = [0]
+
+        o_tiles = {}
+
+        def rep_pair(now):
+            if done[0] >= len(pending):
+                return
+            a_codes, a_scales, born, j, half, a0, na, last = pending[done[0]]
+            if born >= now:
+                return
+            done[0] += 1
+            if a0 == 0:
+                o_tiles[born] = opool.tile([128, 1024], F32, name="o_sb", tag="o_sb")
+            o_sb = o_tiles[born]
+            o = next_bank()
+            for s in range(na):
+                a = half * 4 + a0 + s
+                nc.tensor.matmul_mx(out=o[:, s * 256:(s + 1) * 256],
+                                    lhsT=a_codes[:, s * 128:(s + 1) * 128].bitcast(FP8X4),
+                                    lhsT_scale=a_scales[:, s * 128:(s + 1) * 128],
+                                    rhs=f_codes[:, a * 256:(a + 1) * 256].bitcast(FP8X4),
+                                    rhs_scale=f_scales[:, a * 256:(a + 1) * 256],
+                                    start=True, stop=True)
+            nc.scalar.copy(out=o_sb[:, a0 * 256:(a0 + na) * 256], in_=o[:, 0:na * 256])
+            if last:
+                c0 = half * 1024 + a0 * 256
+                nc.scalar.dma_start(out=out_v[:, j, c0:c0 + na * 256], in_=o_sb[:, a0 * 256:(a0 + na) * 256])
+            elif a0 + na == 4:
+                nc.scalar.dma_start(out=out_v[:, j, half * 1024:(half + 1) * 1024], in_=o_sb[:])
+
+        def quantise_agg(agg, i, a0, na):
+            kind, j0, j1 = jobs[i]
+            a_codes = rpool.tile([128, 256], U32, name="a_codes", tag="a_codes", align_bytes=64)
+            a_scales = rpool.tile([128, 256], U8, name="a_scales", tag="a_scales", align_bytes=64)
+            nc.vector.quantize_mx(out=a_codes[:, 0:na * 128].bitcast(FP8X4), scales=a_scales[:, 0:na * 128],
+                                  in_=agg[:, a0 * 512:(a0 + na) * 512])
+            pending.append((a_codes, a_scales, i, j0, j1, a0, na, i == njobs - 1))
+
+        def regroup(eng, a):
+            src = f_raw[a // 4][:, (a % 4) * 1024:(a % 4 + 1) * 1024].rearrange("p (t c i) -> p c t i", t=4, i=4)
+            dst = f_grp[a // 4][:, (a % 4) * 1024:(a % 4 + 1) * 1024].rearrange("p (c i t) -> p c t i", t=4, i=4)
+            if eng == "s":
+                nc.scalar.copy(out=dst, in_=src)
+            else:
+                nc.vector.tensor_copy(out=dst, in_=src)
+
+        for n in range(XBUFS):
+            load_next()
+
+        g = transpose_unit(0)
+        for r in range(2):
+            quantise_half(g, w_codes[0], w_scales[0], r)
+        g_job = transpose_unit(1)
+        codes = cpool.tile([128, 1024], U32, name="codes", tag="codes", align_bytes=64)
+        scales = cpool.tile([128, 1024], U8, name="scales", tag="scales", align_bytes=64)
+        for r in range(2):
+            quantise_half(g_job, codes, scales, r)
+        g = transpose_unit(2)
+        for r in range(2):
+            quantise_half(g, w_codes[1], w_scales[1], r)
+
+        for i in range(njobs):
+            kind, j0, j1 = jobs[i]
+            if i + 1 < njobs and i > 0:
+                g_next = transpose_unit(i + 3)
+                codes_next = cpool.tile([128, 1024], U32, name="codes", tag="codes", align_bytes=64)
+                scales_next = cpool.tile([128, 1024], U8, name="scales", tag="scales", align_bytes=64)
+            extra = list(REGROUP.get(i, ()))
+            if kind == "edge":
+                agg = apool.tile([128, 2048], BF16, name="agg", tag="agg", align_bytes=64)
+            for aa in range(4):
+                acc = project(0 if kind == "node" else 1, codes, scales, aa)
+                acc_v = acc[:].rearrange("p (t c) -> p c t", t=4)
+                if kind == "node":
+                    j = j0 * 4 + aa
+                    nc.vector.tensor_tensor(out=nodeb[:, j * 512:(j + 1) * 512].rearrange("p (c t) -> p c t", t=4),
+                                            in0=acc_v, in1=bias32[:].unsqueeze(1).to_broadcast([128, 128, 4]), op=ADD)
+                else:
+                    nc.vector.tensor_tensor(out=agg[:, aa * 512:(aa + 1) * 512].rearrange("p (c t) -> p c t", t=4),
+                                            in0=acc_v,
+                                            in1=nodeb[:, j0 * 512:(j0 + 1) * 512].rearrange("p (c t) -> p c t", t=4),
+                                            op=ADD)
+                if aa % 2 == 0 and len(extra) > aa // 2:
+                    regroup(extra[aa // 2][0], extra[aa // 2][1])
+                if aa == 1 and i + 1 < njobs and i > 0:
+                    quantise_half(g_next, codes_next, scales_next, 0)
+                if aa == 3 and i + 1 < njobs and i > 0:
+                    quantise_half(g_next, codes_next, scales_next, 1)
+                if kind == "edge" and i == njobs - 1:
+                    if aa == 1:
+                        quantise_agg(agg, i, 0, 2)
+                    elif aa >= 2:
+                        quantise_agg(agg, i, aa, 1)
+                elif kind == "edge" and aa >= 2:
+                    quantise_agg(agg, i, (aa - 2) * 2, 2)
+                if aa == 3 and i in QF:
+                    h = QF[i]
+                    for r in range(2):
+                        c0 = h * 1024 + r * 512
+                        nc.vector.quantize_mx(out=f_codes[:, c0:c0 + 512].bitcast(FP8X4),
+                                              scales=f_scales[:, c0:c0 + 512],
+                                              in_=f_grp[h][:, r * 2048:(r + 1) * 2048])
+                if i >= RSTART and aa in (LATE_SLOTS if i >= njobs - 2 else RSLOTS):
+                    rep_pair(i)
+            if i == 0:
+                g_next = transpose_unit(3)
+                codes_next = cpool.tile([128, 1024], U32, name="codes", tag="codes", align_bytes=64)
+                scales_next = cpool.tile([128, 1024], U8, name="scales", tag="scales", align_bytes=64)
+                for r in range(2):
+                    quantise_half(g_next, codes_next, scales_next, r)
+            if i + 1 < njobs:
+                codes, scales = codes_next, scales_next
+        for n in range(len(pending) - done[0]):
+            rep_pair(njobs)

@@ -15,13 +15,19 @@ ADD = mybir.AluOpType.add
 B, A, E, P, R = 1024, 8, 1024, 512, 256
 FLOPS = 2 * (B * E * P + B * A * E * P + B * A * P * R)
 
-MANUAL = True
 XBUFS = 6
-REGROUP = {2: (("s", 0), ("s", 1)), 3: (("s", 2), ("s", 3)), 4: (("s", 4), ("s", 5)), 5: (("s", 6), ("s", 7))}
-QF = {4: 0, 6: 1}
+LOOK = 5
+F_LOAD = {6: 0, 7: 1}
+PRE = "vss-"
+PRE_FIRST = 5
+PRE_AT = {}
+STEPS_A = "T P0 A0 x0 P1 A1 q0 x1 P2 A2 x2 g0 P3 A3 q1 x3 g1"
+STEPS_B = "T P0 A0 x0 R P1 A1 q0 x1 R P2 A2 x2 g0 R P3 A3 q1 x3 g1"
+STEPS_C = "T P0 A0 P1 A1 q0 R P2 A2 g0 R P3 A3 q1 g1 R"
+JOB_PLAN = {}
 RSTART = 7
-RSLOTS = (0, 1, 2)
-LATE_SLOTS = (1, 2, 3)
+NREG = {3: 4, 4: 4}
+NFQ = {4: 1, 5: 1, 6: 1, 7: 1}
 
 
 def tile_attributegnn_pa_t_kernel(tc, image_features, edge_attributes, linear_w, linear_b, fwd_proj, out):
@@ -36,14 +42,14 @@ def tile_attributegnn_pa_t_kernel(tc, image_features, edge_attributes, linear_w,
     with ExitStack() as ctx:
         const = ctx.enter_context(tc.tile_pool(name="const", bufs=1))
         xpool = ctx.enter_context(tc.tile_pool(name="xpool", bufs=XBUFS))
+        spool = ctx.enter_context(tc.tile_pool(name="spool", bufs=3))
         gpool = ctx.enter_context(tc.tile_pool(name="gpool", bufs=3))
         cpool = ctx.enter_context(tc.tile_pool(name="cpool", bufs=3))
         apool = ctx.enter_context(tc.tile_pool(name="apool", bufs=3))
         rpool = ctx.enter_context(tc.tile_pool(name="rpool", bufs=16))
         opool = ctx.enter_context(tc.tile_pool(name="opool", bufs=3))
         psum = ctx.enter_context(tc.psum_pool(name="psum", bufs=1))
-        if MANUAL:
-            ctx.enter_context(tc.manual_schedule())
+        ctx.enter_context(tc.manual_schedule())
 
         banks_used = [0]
 
@@ -94,9 +100,27 @@ def tile_attributegnn_pa_t_kernel(tc, image_features, edge_attributes, linear_w,
                 else:
                     nc.sync.dma_start(out=x[:], in_=ea_v[:, j0, j1 * 4096:(j1 + 1) * 4096])
             x_tiles.append(x)
-            if n == 4 or n == 5:
-                h = n - 4
+            if n in F_LOAD:
+                h = F_LOAD[n]
                 nc.sync.dma_start(out=f_raw[h][:].rearrange("p (a s) -> p a s", a=4), in_=f_v[:, h * 4:(h + 1) * 4, :])
+
+        sorted_tiles = {}
+
+        def plan(n):
+            return PRE if n not in PRE_AT else PRE_AT[n]
+
+        def presort(n, aa):
+            if n < PRE_FIRST or n >= len(srcs) or plan(n)[aa] == "-":
+                return
+            if n not in sorted_tiles:
+                sorted_tiles[n] = spool.tile([128, 2048], F32, name="xs", tag="xs")
+            cols = slice(aa * 512, (aa + 1) * 512)
+            dst = sorted_tiles[n][:, cols].rearrange("p (g u c) -> p g u c", g=2, u=2)
+            src = x_tiles[n][:].bitcast(F32)[:, cols].rearrange("p (g c u) -> p g u c", g=2, u=2)
+            if plan(n)[aa] == "s":
+                nc.scalar.copy(out=dst, in_=src)
+            else:
+                nc.vector.tensor_copy(out=dst, in_=src)
 
         def transpose_unit(n):
             x32 = x_tiles[n][:].bitcast(F32)
@@ -105,8 +129,13 @@ def tile_attributegnn_pa_t_kernel(tc, image_features, edge_attributes, linear_w,
             for aa in range(4):
                 xt = next_bank()
                 for s in range(4):
-                    col = aa * 512 + (s // 2) * 256 + s % 2
-                    nc.tensor.transpose(xt[:, s * 128:(s + 1) * 128], x32[:, col:col + 255:2], ident[:])
+                    if n in sorted_tiles and plan(n)[aa] != "-":
+                        col = aa * 512 + s * 128
+                        words = sorted_tiles[n][:, col:col + 128]
+                    else:
+                        col = aa * 512 + (s // 2) * 256 + s % 2
+                        words = x32[:, col:col + 255:2]
+                    nc.tensor.transpose(xt[:, s * 128:(s + 1) * 128], words, ident[:])
                 nc.scalar.copy(out=g32[:, aa // 2, :, aa % 2, :, :],
                                in_=xt[:].rearrange("p (g u c) -> p g c u", g=2, u=2, c=128))
             load_next()
@@ -173,7 +202,9 @@ def tile_attributegnn_pa_t_kernel(tc, image_features, edge_attributes, linear_w,
         def regroup(eng, a):
             src = f_raw[a // 4][:, (a % 4) * 1024:(a % 4 + 1) * 1024].rearrange("p (t c i) -> p c t i", t=4, i=4)
             dst = f_grp[a // 4][:, (a % 4) * 1024:(a % 4 + 1) * 1024].rearrange("p (c i t) -> p c t i", t=4, i=4)
-            if eng == "s":
+            if eng == "g":
+                nc.gpsimd.tensor_scalar(out=dst, in0=src, scalar1=1.0, scalar2=0.0, op0=mybir.AluOpType.mult, op1=ADD)
+            elif eng == "s":
                 nc.scalar.copy(out=dst, in_=src)
             else:
                 nc.vector.tensor_copy(out=dst, in_=src)
@@ -193,55 +224,66 @@ def tile_attributegnn_pa_t_kernel(tc, image_features, edge_attributes, linear_w,
         for r in range(2):
             quantise_half(g, w_codes[1], w_scales[1], r)
 
+        regrouped = [0]
+        fquant = [0]
         for i in range(njobs):
             kind, j0, j1 = jobs[i]
-            if i + 1 < njobs and i > 0:
-                g_next = transpose_unit(i + 3)
-                codes_next = cpool.tile([128, 1024], U32, name="codes", tag="codes", align_bytes=64)
-                scales_next = cpool.tile([128, 1024], U8, name="scales", tag="scales", align_bytes=64)
-            extra = list(REGROUP.get(i, ()))
+            nreg = NREG.get(i, 0)
+            nfq = NFQ.get(i, 0)
             if kind == "edge":
                 agg = apool.tile([128, 2048], BF16, name="agg", tag="agg", align_bytes=64)
-            for aa in range(4):
-                acc = project(0 if kind == "node" else 1, codes, scales, aa)
-                acc_v = acc[:].rearrange("p (t c) -> p c t", t=4)
-                if kind == "node":
-                    j = j0 * 4 + aa
-                    nc.vector.tensor_tensor(out=nodeb[:, j * 512:(j + 1) * 512].rearrange("p (c t) -> p c t", t=4),
-                                            in0=acc_v, in1=bias32[:].unsqueeze(1).to_broadcast([128, 128, 4]), op=ADD)
-                else:
-                    nc.vector.tensor_tensor(out=agg[:, aa * 512:(aa + 1) * 512].rearrange("p (c t) -> p c t", t=4),
-                                            in0=acc_v,
-                                            in1=nodeb[:, j0 * 512:(j0 + 1) * 512].rearrange("p (c t) -> p c t", t=4),
-                                            op=ADD)
-                if aa % 2 == 0 and len(extra) > aa // 2:
-                    regroup(extra[aa // 2][0], extra[aa // 2][1])
-                if aa == 1 and i + 1 < njobs and i > 0:
-                    quantise_half(g_next, codes_next, scales_next, 0)
-                if aa == 3 and i + 1 < njobs and i > 0:
-                    quantise_half(g_next, codes_next, scales_next, 1)
-                if kind == "edge" and i == njobs - 1:
-                    if aa == 1:
-                        quantise_agg(agg, i, 0, 2)
-                    elif aa >= 2:
-                        quantise_agg(agg, i, aa, 1)
-                elif kind == "edge" and aa >= 2:
-                    quantise_agg(agg, i, (aa - 2) * 2, 2)
-                if aa == 3 and i in QF:
-                    h = QF[i]
-                    for r in range(2):
-                        c0 = h * 1024 + r * 512
-                        nc.vector.quantize_mx(out=f_codes[:, c0:c0 + 512].bitcast(FP8X4),
-                                              scales=f_scales[:, c0:c0 + 512],
-                                              in_=f_grp[h][:, r * 2048:(r + 1) * 2048])
-                if i >= RSTART and aa in (LATE_SLOTS if i >= njobs - 2 else RSLOTS):
-                    rep_pair(i)
+            steps = JOB_PLAN.get(i)
+            if steps is None:
+                steps = STEPS_A if i < RSTART else STEPS_B if i < njobs - 2 else STEPS_C
             if i == 0:
-                g_next = transpose_unit(3)
-                codes_next = cpool.tile([128, 1024], U32, name="codes", tag="codes", align_bytes=64)
-                scales_next = cpool.tile([128, 1024], U8, name="scales", tag="scales", align_bytes=64)
-                for r in range(2):
-                    quantise_half(g_next, codes_next, scales_next, r)
+                steps = "P0 A0 P1 A1 P2 A2 P3 A3 T q0 q1 x0 x1 x2 x3"
+            accs = {}
+            for step in steps.split(" "):
+                op = step[0]
+                aa = int(step[1]) if len(step) > 1 else 0
+                if op == "T" and i + 3 < len(srcs):
+                    g_next = transpose_unit(i + 3)
+                    codes_next = cpool.tile([128, 1024], U32, name="codes", tag="codes", align_bytes=64)
+                    scales_next = cpool.tile([128, 1024], U8, name="scales", tag="scales", align_bytes=64)
+                elif op == "P":
+                    accs[aa] = project(0 if kind == "node" else 1, codes, scales, aa)
+                elif op == "A":
+                    acc_v = accs[aa][:].rearrange("p (t c) -> p c t", t=4)
+                    if kind == "node":
+                        j = j0 * 4 + aa
+                        nc.vector.tensor_tensor(out=nodeb[:, j * 512:(j + 1) * 512].rearrange("p (c t) -> p c t", t=4),
+                                                in0=acc_v, in1=bias32[:].unsqueeze(1).to_broadcast([128, 128, 4]), op=ADD)
+                    else:
+                        nc.vector.tensor_tensor(out=agg[:, aa * 512:(aa + 1) * 512].rearrange("p (c t) -> p c t", t=4),
+                                                in0=acc_v,
+                                                in1=nodeb[:, j0 * 512:(j0 + 1) * 512].rearrange("p (c t) -> p c t", t=4),
+                                                op=ADD)
+                    if nreg > 0:
+                        regroup("g", regrouped[0])
+                        regrouped[0] += 1
+                        nreg -= 1
+                elif op == "q" and i + 3 < len(srcs):
+                    quantise_half(g_next, codes_next, scales_next, aa)
+                elif op == "x":
+                    presort(i + LOOK, aa)
+                elif op == "g" and kind == "edge":
+                    if i == njobs - 1:
+                        if aa == 0:
+                            quantise_agg(agg, i, 0, 2)
+                        else:
+                            quantise_agg(agg, i, 2, 1)
+                            quantise_agg(agg, i, 3, 1)
+                    else:
+                        quantise_agg(agg, i, aa * 2, 2)
+                elif op == "R" and i >= RSTART:
+                    rep_pair(i)
+                if op == "q" and nfq > 0:
+                    c0 = fquant[0] * 512
+                    nc.vector.quantize_mx(out=f_codes[:, c0:c0 + 512].bitcast(FP8X4),
+                                          scales=f_scales[:, c0:c0 + 512],
+                                          in_=f_grp[fquant[0] // 2][:, (fquant[0] % 2) * 2048:(fquant[0] % 2 + 1) * 2048])
+                    fquant[0] += 1
+                    nfq -= 1
             if i + 1 < njobs:
                 codes, scales = codes_next, scales_next
         for n in range(len(pending) - done[0]):

@@ -18,16 +18,17 @@ FLOPS = 2 * (B * E * P + B * A * E * P + B * A * P * R)
 XBUFS = 6
 LOOK = 5
 F_LOAD = {6: 0, 7: 1}
-PRE = "vss-"
+PRE = "vvs-"
 PRE_FIRST = 5
-PRE_AT = {}
+PRE_EARLY = "vss-"
+PRE_SWITCH = 12
 STEPS_A = "T P0 A0 x0 P1 A1 q0 x1 P2 A2 x2 g0 P3 A3 q1 x3 g1"
 STEPS_B = "T P0 A0 x0 R P1 A1 q0 x1 R P2 A2 x2 g0 R P3 A3 q1 x3 g1"
 STEPS_C = "T P0 A0 P1 A1 q0 R P2 A2 g0 R P3 A3 q1 g1 R"
-JOB_PLAN = {}
 RSTART = 7
-NREG = {3: 4, 4: 4}
-NFQ = {4: 1, 5: 1, 6: 1, 7: 1}
+RENG = "sv"
+NREG = {3: 2, 4: 2, 5: 2, 6: 2}
+NFQ = {5: 2, 7: 2}
 
 
 def tile_attributegnn_pa_t_kernel(tc, image_features, edge_attributes, linear_w, linear_b, fwd_proj, out):
@@ -107,7 +108,7 @@ def tile_attributegnn_pa_t_kernel(tc, image_features, edge_attributes, linear_w,
         sorted_tiles = {}
 
         def plan(n):
-            return PRE if n not in PRE_AT else PRE_AT[n]
+            return PRE_EARLY if n < PRE_SWITCH else PRE
 
         def presort(n, aa):
             if n < PRE_FIRST or n >= len(srcs) or plan(n)[aa] == "-":
@@ -202,9 +203,7 @@ def tile_attributegnn_pa_t_kernel(tc, image_features, edge_attributes, linear_w,
         def regroup(eng, a):
             src = f_raw[a // 4][:, (a % 4) * 1024:(a % 4 + 1) * 1024].rearrange("p (t c i) -> p c t i", t=4, i=4)
             dst = f_grp[a // 4][:, (a % 4) * 1024:(a % 4 + 1) * 1024].rearrange("p (c i t) -> p c t i", t=4, i=4)
-            if eng == "g":
-                nc.gpsimd.tensor_scalar(out=dst, in0=src, scalar1=1.0, scalar2=0.0, op0=mybir.AluOpType.mult, op1=ADD)
-            elif eng == "s":
+            if eng == "s":
                 nc.scalar.copy(out=dst, in_=src)
             else:
                 nc.vector.tensor_copy(out=dst, in_=src)
@@ -232,9 +231,7 @@ def tile_attributegnn_pa_t_kernel(tc, image_features, edge_attributes, linear_w,
             nfq = NFQ.get(i, 0)
             if kind == "edge":
                 agg = apool.tile([128, 2048], BF16, name="agg", tag="agg", align_bytes=64)
-            steps = JOB_PLAN.get(i)
-            if steps is None:
-                steps = STEPS_A if i < RSTART else STEPS_B if i < njobs - 2 else STEPS_C
+            steps = STEPS_A if i < RSTART else STEPS_B if i < njobs - 2 else STEPS_C
             if i == 0:
                 steps = "P0 A0 P1 A1 P2 A2 P3 A3 T q0 q1 x0 x1 x2 x3"
             accs = {}
@@ -259,7 +256,7 @@ def tile_attributegnn_pa_t_kernel(tc, image_features, edge_attributes, linear_w,
                                                 in1=nodeb[:, j0 * 512:(j0 + 1) * 512].rearrange("p (c t) -> p c t", t=4),
                                                 op=ADD)
                     if nreg > 0:
-                        regroup("g", regrouped[0])
+                        regroup(RENG[regrouped[0] % len(RENG)], regrouped[0])
                         regrouped[0] += 1
                         nreg -= 1
                 elif op == "q" and i + 3 < len(srcs):

@@ -18,17 +18,19 @@ FLOPS = 2 * (B * E * P + B * A * E * P + B * A * P * R)
 XBUFS = 6
 LOOK = 5
 F_LOAD = {6: 0, 7: 1}
-PRE = "vvs-"
+PRE = "vs--"
 PRE_FIRST = 5
-PRE_EARLY = "vss-"
-PRE_SWITCH = 12
-STEPS_A = "T P0 A0 x0 P1 A1 q0 x1 P2 A2 x2 g0 P3 A3 q1 x3 g1"
-STEPS_B = "T P0 A0 x0 R P1 A1 q0 x1 R P2 A2 x2 g0 R P3 A3 q1 x3 g1"
+HEAD = 0
+PRE_HEAD = "vvvv"
+PRE_EARLY = "s---"
+PRE_SWITCH = 14
+STEPS_A = "T P0 A0 x0 P1 A1 Q x1 P2 A2 x2 P3 A3 x3 G"
+STEPS_B = "T P0 A0 x0 R P1 A1 Q x1 R P2 A2 x2 R P3 A3 x3 G"
 STEPS_C = "T P0 A0 P1 A1 q0 R P2 A2 g0 R P3 A3 q1 g1 R"
-RSTART = 7
-RENG = "sv"
+RSTART = 8
+RENG = "ssv"
 NREG = {3: 2, 4: 2, 5: 2, 6: 2}
-NFQ = {5: 2, 7: 2}
+NFQ = {5: 1, 6: 1, 7: 1, 8: 1}
 
 
 def tile_attributegnn_pa_t_kernel(tc, image_features, edge_attributes, linear_w, linear_b, fwd_proj, out):
@@ -47,7 +49,7 @@ def tile_attributegnn_pa_t_kernel(tc, image_features, edge_attributes, linear_w,
         gpool = ctx.enter_context(tc.tile_pool(name="gpool", bufs=3))
         cpool = ctx.enter_context(tc.tile_pool(name="cpool", bufs=3))
         apool = ctx.enter_context(tc.tile_pool(name="apool", bufs=3))
-        rpool = ctx.enter_context(tc.tile_pool(name="rpool", bufs=16))
+        rpool = ctx.enter_context(tc.tile_pool(name="rpool", bufs=9))
         opool = ctx.enter_context(tc.tile_pool(name="opool", bufs=3))
         psum = ctx.enter_context(tc.psum_pool(name="psum", bufs=1))
         ctx.enter_context(tc.manual_schedule())
@@ -108,6 +110,8 @@ def tile_attributegnn_pa_t_kernel(tc, image_features, edge_attributes, linear_w,
         sorted_tiles = {}
 
         def plan(n):
+            if n < HEAD:
+                return PRE_HEAD
             return PRE_EARLY if n < PRE_SWITCH else PRE
 
         def presort(n, aa):
@@ -128,6 +132,8 @@ def tile_attributegnn_pa_t_kernel(tc, image_features, edge_attributes, linear_w,
             g = gpool.tile([128, 4096], BF16, name="g", tag="g", align_bytes=64)
             g32 = g[:].bitcast(F32).rearrange("p (r g a c u) -> p r g a c u", r=2, g=2, a=2, c=128, u=2)
             for aa in range(4):
+                if n < HEAD:
+                    presort(n, aa)
                 xt = next_bank()
                 for s in range(4):
                     if n in sorted_tiles and plan(n)[aa] != "-":
@@ -194,11 +200,15 @@ def tile_attributegnn_pa_t_kernel(tc, image_features, edge_attributes, linear_w,
 
         def quantise_agg(agg, i, a0, na):
             kind, j0, j1 = jobs[i]
-            a_codes = rpool.tile([128, 256], U32, name="a_codes", tag="a_codes", align_bytes=64)
-            a_scales = rpool.tile([128, 256], U8, name="a_scales", tag="a_scales", align_bytes=64)
+            a_codes = rpool.tile([128, 512], U32, name="a_codes", tag="a_codes", align_bytes=64)
+            a_scales = rpool.tile([128, 512], U8, name="a_scales", tag="a_scales", align_bytes=64)
             nc.vector.quantize_mx(out=a_codes[:, 0:na * 128].bitcast(FP8X4), scales=a_scales[:, 0:na * 128],
                                   in_=agg[:, a0 * 512:(a0 + na) * 512])
-            pending.append((a_codes, a_scales, i, j0, j1, a0, na, i == njobs - 1))
+            if na == 4:
+                for b0 in (0, 2):
+                    pending.append((a_codes[:, b0 * 128:(b0 + 2) * 128], a_scales[:, b0 * 128:(b0 + 2) * 128], i, j0, j1, b0, 2, False))
+            else:
+                pending.append((a_codes, a_scales, i, j0, j1, a0, na, i == njobs - 1))
 
         def regroup(eng, a):
             src = f_raw[a // 4][:, (a % 4) * 1024:(a % 4 + 1) * 1024].rearrange("p (t c i) -> p c t i", t=4, i=4)
@@ -259,6 +269,10 @@ def tile_attributegnn_pa_t_kernel(tc, image_features, edge_attributes, linear_w,
                         regroup(RENG[regrouped[0] % len(RENG)], regrouped[0])
                         regrouped[0] += 1
                         nreg -= 1
+                elif op == "Q" and i + 3 < len(srcs):
+                    nc.vector.quantize_mx(out=codes_next[:].bitcast(FP8X4), scales=scales_next[:], in_=g_next[:])
+                elif op == "G" and kind == "edge":
+                    quantise_agg(agg, i, 0, 4)
                 elif op == "q" and i + 3 < len(srcs):
                     quantise_half(g_next, codes_next, scales_next, aa)
                 elif op == "x":
@@ -274,7 +288,7 @@ def tile_attributegnn_pa_t_kernel(tc, image_features, edge_attributes, linear_w,
                         quantise_agg(agg, i, aa * 2, 2)
                 elif op == "R" and i >= RSTART:
                     rep_pair(i)
-                if op == "q" and nfq > 0:
+                if op in "qQ" and nfq > 0:
                     c0 = fquant[0] * 512
                     nc.vector.quantize_mx(out=f_codes[:, c0:c0 + 512].bitcast(FP8X4),
                                           scales=f_scales[:, c0:c0 + 512],

@@ -18,15 +18,18 @@ FLOPS = 2 * (B * E * P + B * A * E * P + B * A * P * R)
 XBUFS = 6
 LOOK = 5
 F_LOAD = {6: 0, 7: 1}
-PRE = "vs--"
+PRE = "vvs-"
 PRE_FIRST = 5
 HEAD = 0
 PRE_HEAD = "vvvv"
+PRE_A = "s---"
+SW_A = 9
 PRE_EARLY = "s---"
-PRE_SWITCH = 14
-STEPS_A = "T P0 A0 x0 P1 A1 Q x1 P2 A2 x2 P3 A3 x3 G"
-STEPS_B = "T P0 A0 x0 R P1 A1 Q x1 R P2 A2 x2 R P3 A3 x3 G"
-STEPS_C = "T P0 A0 P1 A1 q0 R P2 A2 g0 R P3 A3 q1 g1 R"
+PRE_SWITCH = 15
+STEPS_A = "T P0 A0 x0 P1 A1 q0 x1 P2 A2 x2 P3 A3 q1 x3 G"
+STEPS_B = "T P0 A0 x0 R P1 A1 q0 x1 R P2 A2 x2 R P3 A3 q1 x3 G"
+STEPS_C = "T P0 A0 R P1 A1 q0 R P2 A2 R P3 A3 q1 G"
+STEPS_D = "P0 A0 P1 A1 R P2 A2 g0 R P3 A3 g2 g3 R"
 RSTART = 8
 RENG = "ssv"
 NREG = {3: 2, 4: 2, 5: 2, 6: 2}
@@ -112,7 +115,7 @@ def tile_attributegnn_pa_t_kernel(tc, image_features, edge_attributes, linear_w,
         def plan(n):
             if n < HEAD:
                 return PRE_HEAD
-            return PRE_EARLY if n < PRE_SWITCH else PRE
+            return PRE_A if n < SW_A else PRE_EARLY if n < PRE_SWITCH else PRE
 
         def presort(n, aa):
             if n < PRE_FIRST or n >= len(srcs) or plan(n)[aa] == "-":
@@ -194,9 +197,9 @@ def tile_attributegnn_pa_t_kernel(tc, image_features, edge_attributes, linear_w,
             nc.scalar.copy(out=o_sb[:, a0 * 256:(a0 + na) * 256], in_=o[:, 0:na * 256])
             if last:
                 c0 = half * 1024 + a0 * 256
-                nc.scalar.dma_start(out=out_v[:, j, c0:c0 + na * 256], in_=o_sb[:, a0 * 256:(a0 + na) * 256])
+                nc.sync.dma_start(out=out_v[:, j, c0:c0 + na * 256], in_=o_sb[:, a0 * 256:(a0 + na) * 256])
             elif a0 + na == 4:
-                nc.scalar.dma_start(out=out_v[:, j, half * 1024:(half + 1) * 1024], in_=o_sb[:])
+                nc.sync.dma_start(out=out_v[:, j, half * 1024:(half + 1) * 1024], in_=o_sb[:])
 
         def quantise_agg(agg, i, a0, na):
             kind, j0, j1 = jobs[i]
@@ -241,7 +244,7 @@ def tile_attributegnn_pa_t_kernel(tc, image_features, edge_attributes, linear_w,
             nfq = NFQ.get(i, 0)
             if kind == "edge":
                 agg = apool.tile([128, 2048], BF16, name="agg", tag="agg", align_bytes=64)
-            steps = STEPS_A if i < RSTART else STEPS_B if i < njobs - 2 else STEPS_C
+            steps = STEPS_A if i < RSTART else STEPS_B if i < njobs - 2 else STEPS_C if i == njobs - 2 else STEPS_D
             if i == 0:
                 steps = "P0 A0 P1 A1 P2 A2 P3 A3 T q0 q1 x0 x1 x2 x3"
             accs = {}
@@ -269,8 +272,6 @@ def tile_attributegnn_pa_t_kernel(tc, image_features, edge_attributes, linear_w,
                         regroup(RENG[regrouped[0] % len(RENG)], regrouped[0])
                         regrouped[0] += 1
                         nreg -= 1
-                elif op == "Q" and i + 3 < len(srcs):
-                    nc.vector.quantize_mx(out=codes_next[:].bitcast(FP8X4), scales=scales_next[:], in_=g_next[:])
                 elif op == "G" and kind == "edge":
                     quantise_agg(agg, i, 0, 4)
                 elif op == "q" and i + 3 < len(srcs):
@@ -279,11 +280,7 @@ def tile_attributegnn_pa_t_kernel(tc, image_features, edge_attributes, linear_w,
                     presort(i + LOOK, aa)
                 elif op == "g" and kind == "edge":
                     if i == njobs - 1:
-                        if aa == 0:
-                            quantise_agg(agg, i, 0, 2)
-                        else:
-                            quantise_agg(agg, i, 2, 1)
-                            quantise_agg(agg, i, 3, 1)
+                        quantise_agg(agg, i, aa, 2 if aa == 0 else 1)
                     else:
                         quantise_agg(agg, i, aa * 2, 2)
                 elif op == "R" and i >= RSTART:

@@ -258,15 +258,15 @@ def tile_attributegnn_pa_t_kernel(tc, image_features, edge_attributes, linear_w,
                 elif op == "P":
                     accs[aa] = project(0 if kind == "node" else 1, codes, scales, aa)
                 elif op == "A":
-                    acc_v = accs[aa][:].rearrange("p (t c) -> p c t", t=4)
+                    acc_v = accs[aa][:].rearrange("p (t c i) -> p c t i", t=4, i=4)
                     if kind == "node":
                         j = j0 * 4 + aa
-                        nc.vector.tensor_tensor(out=nodeb[:, j * 512:(j + 1) * 512].rearrange("p (c t) -> p c t", t=4),
-                                                in0=acc_v, in1=bias32[:].unsqueeze(1).to_broadcast([128, 128, 4]), op=ADD)
+                        nc.vector.tensor_tensor(out=nodeb[:, j * 512:(j + 1) * 512].rearrange("p (c t i) -> p c t i", t=4, i=4),
+                                                in0=acc_v, in1=bias32[:].unsqueeze(1).unsqueeze(3).to_broadcast([128, 32, 4, 4]), op=ADD)
                     else:
-                        nc.vector.tensor_tensor(out=agg[:, aa * 512:(aa + 1) * 512].rearrange("p (c t) -> p c t", t=4),
+                        nc.vector.tensor_tensor(out=agg[:, aa * 512:(aa + 1) * 512].rearrange("p (c i t) -> p c t i", t=4, i=4),
                                                 in0=acc_v,
-                                                in1=nodeb[:, j0 * 512:(j0 + 1) * 512].rearrange("p (c t) -> p c t", t=4),
+                                                in1=nodeb[:, j0 * 512:(j0 + 1) * 512].rearrange("p (c t i) -> p c t i", t=4, i=4),
                                                 op=ADD)
                     if nreg > 0:
                         regroup(RENG[regrouped[0] % len(RENG)], regrouped[0])

@@ -26,9 +26,9 @@ PRE_A = "s---"
 SW_A = 9
 PRE_EARLY = "s---"
 PRE_SWITCH = 15
-STEPS_A = "T P0 A0 x0 P1 A1 q0 x1 P2 A2 x2 P3 A3 q1 x3 G"
-STEPS_B = "T P0 A0 x0 R P1 A1 q0 x1 R P2 A2 x2 R P3 A3 q1 x3 G"
-STEPS_C = "T P0 A0 R P1 A1 q0 R P2 A2 R P3 A3 q1 G"
+STEPS_A = "S P0 A0 x0 P1 A1 q0 x1 U P2 A2 x2 P3 A3 q1 x3 G"
+STEPS_B = "S P0 A0 x0 R P1 A1 q0 x1 R U P2 A2 x2 R P3 A3 q1 x3 G"
+STEPS_C = "S P0 A0 R P1 A1 q0 R U P2 A2 R P3 A3 q1 G"
 STEPS_D = "P0 A0 P1 A1 R P2 A2 g0 R P3 A3 g2 g3 R"
 RSTART = 8
 RENG = "ssv"
@@ -130,11 +130,12 @@ def tile_attributegnn_pa_t_kernel(tc, image_features, edge_attributes, linear_w,
             else:
                 nc.vector.tensor_copy(out=dst, in_=src)
 
-        def transpose_unit(n):
+        def transpose_unit(n, strips=(0, 1, 2, 3), g=None):
             x32 = x_tiles[n][:].bitcast(F32)
-            g = gpool.tile([128, 4096], BF16, name="g", tag="g", align_bytes=64)
+            if g is None:
+                g = gpool.tile([128, 4096], BF16, name="g", tag="g", align_bytes=64)
             g32 = g[:].bitcast(F32).rearrange("p (r g a c u) -> p r g a c u", r=2, g=2, a=2, c=128, u=2)
-            for aa in range(4):
+            for aa in strips:
                 if n < HEAD:
                     presort(n, aa)
                 xt = next_bank()
@@ -148,7 +149,8 @@ def tile_attributegnn_pa_t_kernel(tc, image_features, edge_attributes, linear_w,
                     nc.tensor.transpose(xt[:, s * 128:(s + 1) * 128], words, ident[:])
                 nc.scalar.copy(out=g32[:, aa // 2, :, aa % 2, :, :],
                                in_=xt[:].rearrange("p (g u c) -> p g c u", g=2, u=2, c=128))
-            load_next()
+            if 3 in strips:
+                load_next()
             return g
 
         def quantise_half(g, codes, scales, r):
@@ -251,8 +253,10 @@ def tile_attributegnn_pa_t_kernel(tc, image_features, edge_attributes, linear_w,
             for step in steps.split(" "):
                 op = step[0]
                 aa = int(step[1]) if len(step) > 1 else 0
-                if op == "T" and i + 3 < len(srcs):
-                    g_next = transpose_unit(i + 3)
+                if op == "U" and i + 3 < len(srcs):
+                    transpose_unit(i + 3, (2, 3), g_next)
+                elif op in "TS" and i + 3 < len(srcs):
+                    g_next = transpose_unit(i + 3, (0, 1) if op == "S" else (0, 1, 2, 3))
                     codes_next = cpool.tile([128, 1024], U32, name="codes", tag="codes", align_bytes=64)
                     scales_next = cpool.tile([128, 1024], U8, name="scales", tag="scales", align_bytes=64)
                 elif op == "P":

@@ -15,45 +15,42 @@ ADD = mybir.AluOpType.add
 B, A, E, P, R = 1024, 8, 1024, 512, 256
 FLOPS = 2 * (B * E * P + B * A * E * P + B * A * P * R)
 
-XBUFS = 6
-LOOK = 5
-F_LOAD = {6: 0, 7: 1}
-PRE = "vvs-"
-PRE_FIRST = 5
-HEAD = 0
-PRE_HEAD = "vvvv"
-PRE_A = "s---"
-SW_A = 9
-PRE_EARLY = "s---"
-PRE_SWITCH = 15
-STEPS_A = "S P0 A0 x0 P1 A1 q0 x1 U P2 A2 x2 P3 A3 q1 x3 G"
-STEPS_B = "S P0 A0 x0 R P1 A1 q0 x1 R U P2 A2 x2 R P3 A3 q1 x3 G"
-STEPS_C = "S P0 A0 R P1 A1 q0 R U P2 A2 R P3 A3 q1 G"
-STEPS_D = "P0 A0 P1 A1 R P2 A2 g0 R P3 A3 g2 g3 R"
-RSTART = 8
-RENG = "ssv"
-NREG = {3: 2, 4: 2, 5: 2, 6: 2}
-NFQ = {5: 1, 6: 1, 7: 1, 8: 1}
+LOADS_AHEAD = 6
+SORT_AHEAD = 5
+FIRST_SORTED = 5
+FIRST_LATE = 15
+FWD_PROJ_BEHIND = {6: 0, 7: 1}
+REGROUP_JOBS = (3, 4, 5, 6)
+QUANTISE_JOBS = (5, 6, 7, 8)
+FIRST_SECOND = 8
+
+
+def sorter(n, strip):
+    if n < FIRST_SORTED:
+        return None
+    if n < FIRST_LATE:
+        return ("scalar", None, "scalar", None)[strip]
+    return ("vector", "vector", "scalar", None)[strip]
 
 
 def tile_attributegnn_pa_t_kernel(tc, image_features, edge_attributes, linear_w, linear_b, fwd_proj, out):
     nc = tc.nc
     w_v = linear_w.rearrange("(q t) (h k) -> h q t k", t=4, h=2)
-    img_v = image_features.rearrange("(c j) k -> c (j k)", j=8)
-    ea_v = edge_attributes.rearrange("(c j) a k -> c j (a k)", j=8)
+    image_v = image_features.rearrange("(c j) k -> c (j k)", j=8)
+    edge_v = edge_attributes.rearrange("(c j) a k -> c j (a k)", j=8)
     f_v = fwd_proj.rearrange("a (q t) r -> q a (t r)", t=4)
     out_v = out.rearrange("(c j) a r -> c j (a r)", j=8)
     b_v = linear_b.rearrange("(q t) -> q t", t=4)
 
     with ExitStack() as ctx:
         const = ctx.enter_context(tc.tile_pool(name="const", bufs=1))
-        xpool = ctx.enter_context(tc.tile_pool(name="xpool", bufs=XBUFS))
-        spool = ctx.enter_context(tc.tile_pool(name="spool", bufs=3))
-        gpool = ctx.enter_context(tc.tile_pool(name="gpool", bufs=3))
-        cpool = ctx.enter_context(tc.tile_pool(name="cpool", bufs=3))
-        apool = ctx.enter_context(tc.tile_pool(name="apool", bufs=3))
-        rpool = ctx.enter_context(tc.tile_pool(name="rpool", bufs=9))
-        opool = ctx.enter_context(tc.tile_pool(name="opool", bufs=3))
+        load_pool = ctx.enter_context(tc.tile_pool(name="load_pool", bufs=LOADS_AHEAD))
+        sort_pool = ctx.enter_context(tc.tile_pool(name="sort_pool", bufs=3))
+        turn_pool = ctx.enter_context(tc.tile_pool(name="turn_pool", bufs=3))
+        code_pool = ctx.enter_context(tc.tile_pool(name="code_pool", bufs=3))
+        agg_pool = ctx.enter_context(tc.tile_pool(name="agg_pool", bufs=3))
+        agg_code_pool = ctx.enter_context(tc.tile_pool(name="agg_code_pool", bufs=9))
+        out_pool = ctx.enter_context(tc.tile_pool(name="out_pool", bufs=3))
         psum = ctx.enter_context(tc.psum_pool(name="psum", bufs=1))
         ctx.enter_context(tc.manual_schedule())
 
@@ -71,232 +68,228 @@ def tile_attributegnn_pa_t_kernel(tc, image_features, edge_attributes, linear_w,
             nc.scalar.dma_start(out=bias_bf[:], in_=b_v)
         bias32 = const.tile([128, 4], F32, name="bias32")
         nc.vector.tensor_copy(out=bias32[:], in_=bias_bf[:])
-        nodeb = const.tile([128, 4096], F32, name="nodeb")
+        node_sums = const.tile([128, 4096], F32, name="node_sums")
         w_codes = [const.tile([128, 1024], U32, name="w_codes%d" % h, align_bytes=64) for h in range(2)]
         w_scales = [const.tile([128, 1024], U8, name="w_scales%d" % h, align_bytes=64) for h in range(2)]
         f_codes = const.tile([128, 2048], U32, name="f_codes", align_bytes=64)
         f_scales = const.tile([128, 2048], U8, name="f_scales", align_bytes=64)
         f_raw = [const.tile([128, 4096], BF16, name="f_raw%d" % h) for h in range(2)]
-        f_grp = [const.tile([128, 4096], BF16, name="f_grp%d" % h, align_bytes=64) for h in range(2)]
+        f_grouped = [const.tile([128, 4096], BF16, name="f_grouped%d" % h, align_bytes=64) for h in range(2)]
 
-        jobs = [("node", 0, 0)] + [("edge", u // 2, u % 2) for u in range(8)]
-        jobs = jobs + [("node", 1, 0)] + [("edge", u // 2, u % 2) for u in range(8, 16)]
+        jobs = []
+        for quad in range(2):
+            jobs.append(("node", quad, 0))
+            jobs.extend([("edge", 4 * quad + u // 2, u % 2) for u in range(8)])
         njobs = len(jobs)
+        last = njobs - 1
 
-        srcs = [("w", 0), ("job", 0), ("w", 1)] + [("job", i) for i in range(1, njobs)]
-        x_tiles = []
+        sources = [("w", 0), ("job", 0), ("w", 1)] + [("job", i) for i in range(1, njobs)]
+        loaded = []
 
         def load_next():
-            n = len(x_tiles)
-            if n >= len(srcs):
+            n = len(loaded)
+            if n >= len(sources):
                 return
-            kind, idx = srcs[n]
-            x = xpool.tile([128, 4096], BF16, name="x", tag="x")
+            kind, idx = sources[n]
+            x = load_pool.tile([128, 4096], BF16, name="x", tag="x")
             if kind == "w":
                 for t in range(4):
                     nc.sync.dma_start(out=x[:, t * 1024:(t + 1) * 1024], in_=w_v[idx][:, t, :])
             else:
-                jk, j0, j1 = jobs[idx]
-                if jk == "node" and n < 3:
+                job_kind, j, half = jobs[idx]
+                if idx == 0:
                     for t in range(4):
-                        c0 = j0 * 4096 + t * 1024
-                        nc.sync.dma_start(out=x[:, t * 1024:(t + 1) * 1024], in_=img_v[:, c0:c0 + 1024])
-                elif jk == "node":
-                    nc.sync.dma_start(out=x[:], in_=img_v[:, j0 * 4096:(j0 + 1) * 4096])
+                        nc.sync.dma_start(out=x[:, t * 1024:(t + 1) * 1024], in_=image_v[:, t * 1024:(t + 1) * 1024])
+                elif job_kind == "node":
+                    nc.sync.dma_start(out=x[:], in_=image_v[:, j * 4096:(j + 1) * 4096])
                 else:
-                    nc.sync.dma_start(out=x[:], in_=ea_v[:, j0, j1 * 4096:(j1 + 1) * 4096])
-            x_tiles.append(x)
-            if n in F_LOAD:
-                h = F_LOAD[n]
+                    nc.sync.dma_start(out=x[:], in_=edge_v[:, j, half * 4096:(half + 1) * 4096])
+            loaded.append(x)
+            if n in FWD_PROJ_BEHIND:
+                h = FWD_PROJ_BEHIND[n]
                 nc.sync.dma_start(out=f_raw[h][:].rearrange("p (a s) -> p a s", a=4), in_=f_v[:, h * 4:(h + 1) * 4, :])
 
         sorted_tiles = {}
 
-        def plan(n):
-            if n < HEAD:
-                return PRE_HEAD
-            return PRE_A if n < SW_A else PRE_EARLY if n < PRE_SWITCH else PRE
-
-        def presort(n, aa):
-            if n < PRE_FIRST or n >= len(srcs) or plan(n)[aa] == "-":
+        def sort_strip(n, strip):
+            if n >= len(sources) or sorter(n, strip) is None:
                 return
             if n not in sorted_tiles:
-                sorted_tiles[n] = spool.tile([128, 2048], F32, name="xs", tag="xs")
-            cols = slice(aa * 512, (aa + 1) * 512)
+                sorted_tiles[n] = sort_pool.tile([128, 2048], F32, name="sorted_words", tag="sorted_words")
+            cols = slice(strip * 512, (strip + 1) * 512)
             dst = sorted_tiles[n][:, cols].rearrange("p (g u c) -> p g u c", g=2, u=2)
-            src = x_tiles[n][:].bitcast(F32)[:, cols].rearrange("p (g c u) -> p g u c", g=2, u=2)
-            if plan(n)[aa] == "s":
+            src = loaded[n][:].bitcast(F32)[:, cols].rearrange("p (g c u) -> p g u c", g=2, u=2)
+            if sorter(n, strip) == "scalar":
                 nc.scalar.copy(out=dst, in_=src)
             else:
                 nc.vector.tensor_copy(out=dst, in_=src)
 
-        def transpose_unit(n, strips=(0, 1, 2, 3), g=None):
-            x32 = x_tiles[n][:].bitcast(F32)
-            if g is None:
-                g = gpool.tile([128, 4096], BF16, name="g", tag="g", align_bytes=64)
-            g32 = g[:].bitcast(F32).rearrange("p (r g a c u) -> p r g a c u", r=2, g=2, a=2, c=128, u=2)
-            for aa in strips:
-                if n < HEAD:
-                    presort(n, aa)
-                xt = next_bank()
+        turned = {}
+
+        def transpose_strips(n, strips):
+            if n not in turned:
+                turned[n] = turn_pool.tile([128, 4096], BF16, name="turned", tag="turned", align_bytes=64)
+            words = loaded[n][:].bitcast(F32)
+            turned_words = turned[n][:].bitcast(F32).rearrange("p (r g a c u) -> p r g a c u", r=2, g=2, a=2, c=128, u=2)
+            for strip in strips:
+                bank = next_bank()
                 for s in range(4):
-                    if n in sorted_tiles and plan(n)[aa] != "-":
-                        col = aa * 512 + s * 128
-                        words = sorted_tiles[n][:, col:col + 128]
+                    g, u = s // 2, s % 2
+                    if sorter(n, strip) is None:
+                        col = strip * 512 + g * 256 + u
+                        part = words[:, col:col + 255:2]
                     else:
-                        col = aa * 512 + (s // 2) * 256 + s % 2
-                        words = x32[:, col:col + 255:2]
-                    nc.tensor.transpose(xt[:, s * 128:(s + 1) * 128], words, ident[:])
-                nc.scalar.copy(out=g32[:, aa // 2, :, aa % 2, :, :],
-                               in_=xt[:].rearrange("p (g u c) -> p g c u", g=2, u=2, c=128))
+                        col = strip * 512 + s * 128
+                        part = sorted_tiles[n][:, col:col + 128]
+                    nc.tensor.transpose(bank[:, s * 128:(s + 1) * 128], part, ident[:])
+                nc.scalar.copy(out=turned_words[:, strip // 2, :, strip % 2, :, :],
+                               in_=bank[:].rearrange("p (g u c) -> p g c u", g=2, u=2, c=128))
             if 3 in strips:
                 load_next()
-            return g
 
-        def quantise_half(g, codes, scales, r):
+        def quantise_half(n, codes, scales, r):
             nc.vector.quantize_mx(out=codes[:, r * 512:(r + 1) * 512].bitcast(FP8X4),
                                   scales=scales[:, r * 512:(r + 1) * 512],
-                                  in_=g[:, r * 2048:(r + 1) * 2048])
+                                  in_=turned[n][:, r * 2048:(r + 1) * 2048])
 
-        def project(h, codes, scales, aa):
+        def new_codes():
+            codes = code_pool.tile([128, 1024], U32, name="codes", tag="codes", align_bytes=64)
+            scales = code_pool.tile([128, 1024], U8, name="scales", tag="scales", align_bytes=64)
+            return codes, scales
+
+        def project(h, codes, scales, strip):
             acc = next_bank()
             for t in range(4):
-                for gi in range(2):
-                    wc = (t // 2) * 512 + gi * 256 + (t % 2) * 128
-                    dc = (aa // 2) * 512 + gi * 256 + (aa % 2) * 128
+                for g in range(2):
+                    wc = (t // 2) * 512 + g * 256 + (t % 2) * 128
+                    dc = (strip // 2) * 512 + g * 256 + (strip % 2) * 128
                     nc.tensor.matmul_mx(out=acc[:, t * 128:(t + 1) * 128],
                                         lhsT=w_codes[h][:, wc:wc + 128].bitcast(FP8X4),
                                         lhsT_scale=w_scales[h][:, wc:wc + 128],
                                         rhs=codes[:, dc:dc + 128].bitcast(FP8X4),
                                         rhs_scale=scales[:, dc:dc + 128],
-                                        start=(gi == 0), stop=(gi == 1))
+                                        start=(g == 0), stop=(g == 1))
             return acc
 
-        pending = []
-        done = [0]
+        def add_out(acc, i, strip, agg):
+            kind, j, half = jobs[i]
+            acc_v = acc[:].rearrange("p (t c i) -> p c t i", t=4, i=4)
+            if kind == "node":
+                j = j * 4 + strip
+                nc.vector.tensor_tensor(out=node_sums[:, j * 512:(j + 1) * 512].rearrange("p (c t i) -> p c t i", t=4, i=4),
+                                        in0=acc_v,
+                                        in1=bias32[:].unsqueeze(1).unsqueeze(3).to_broadcast([128, 32, 4, 4]),
+                                        op=ADD)
+            else:
+                nc.vector.tensor_tensor(out=agg[:, strip * 512:(strip + 1) * 512].rearrange("p (c i t) -> p c t i", t=4, i=4),
+                                        in0=acc_v,
+                                        in1=node_sums[:, j * 512:(j + 1) * 512].rearrange("p (c t i) -> p c t i", t=4, i=4),
+                                        op=ADD)
 
-        o_tiles = {}
+        waiting = []
+        out_tiles = {}
 
-        def rep_pair(now):
-            if done[0] >= len(pending):
+        def quantise_agg(agg, i, first, count):
+            codes = agg_code_pool.tile([128, 512], U32, name="agg_codes", tag="agg_codes", align_bytes=64)
+            scales = agg_code_pool.tile([128, 512], U8, name="agg_scales", tag="agg_scales", align_bytes=64)
+            nc.vector.quantize_mx(out=codes[:, 0:count * 128].bitcast(FP8X4), scales=scales[:, 0:count * 128],
+                                  in_=agg[:, first * 512:(first + count) * 512])
+            for k in range(0, count, 2):
+                pair = min(2, count - k)
+                cols = slice(k * 128, (k + pair) * 128)
+                waiting.append((codes[:, cols], scales[:, cols], i, first + k, pair))
+
+        def second_product(before):
+            if not waiting or waiting[0][2] >= before:
                 return
-            a_codes, a_scales, born, j, half, a0, na, last = pending[done[0]]
-            if born >= now:
-                return
-            done[0] += 1
-            if a0 == 0:
-                o_tiles[born] = opool.tile([128, 1024], F32, name="o_sb", tag="o_sb")
-            o_sb = o_tiles[born]
-            o = next_bank()
-            for s in range(na):
-                a = half * 4 + a0 + s
-                nc.tensor.matmul_mx(out=o[:, s * 256:(s + 1) * 256],
-                                    lhsT=a_codes[:, s * 128:(s + 1) * 128].bitcast(FP8X4),
-                                    lhsT_scale=a_scales[:, s * 128:(s + 1) * 128],
+            codes, scales, i, first, count = waiting.pop(0)
+            kind, j, half = jobs[i]
+            if first == 0:
+                out_tiles[i] = out_pool.tile([128, 1024], F32, name="out_tile", tag="out_tile")
+            o = out_tiles[i]
+            bank = next_bank()
+            for s in range(count):
+                a = half * 4 + first + s
+                nc.tensor.matmul_mx(out=bank[:, s * 256:(s + 1) * 256],
+                                    lhsT=codes[:, s * 128:(s + 1) * 128].bitcast(FP8X4),
+                                    lhsT_scale=scales[:, s * 128:(s + 1) * 128],
                                     rhs=f_codes[:, a * 256:(a + 1) * 256].bitcast(FP8X4),
                                     rhs_scale=f_scales[:, a * 256:(a + 1) * 256],
                                     start=True, stop=True)
-            nc.scalar.copy(out=o_sb[:, a0 * 256:(a0 + na) * 256], in_=o[:, 0:na * 256])
-            if last:
-                c0 = half * 1024 + a0 * 256
-                nc.sync.dma_start(out=out_v[:, j, c0:c0 + na * 256], in_=o_sb[:, a0 * 256:(a0 + na) * 256])
-            elif a0 + na == 4:
-                nc.sync.dma_start(out=out_v[:, j, half * 1024:(half + 1) * 1024], in_=o_sb[:])
+            end = first + count
+            nc.scalar.copy(out=o[:, first * 256:end * 256], in_=bank[:, 0:count * 256])
+            if i == last:
+                nc.sync.dma_start(out=out_v[:, j, half * 1024 + first * 256:half * 1024 + end * 256],
+                                  in_=o[:, first * 256:end * 256])
+            elif end == 4:
+                nc.sync.dma_start(out=out_v[:, j, half * 1024:(half + 1) * 1024], in_=o[:])
 
-        def quantise_agg(agg, i, a0, na):
-            kind, j0, j1 = jobs[i]
-            a_codes = rpool.tile([128, 512], U32, name="a_codes", tag="a_codes", align_bytes=64)
-            a_scales = rpool.tile([128, 512], U8, name="a_scales", tag="a_scales", align_bytes=64)
-            nc.vector.quantize_mx(out=a_codes[:, 0:na * 128].bitcast(FP8X4), scales=a_scales[:, 0:na * 128],
-                                  in_=agg[:, a0 * 512:(a0 + na) * 512])
-            if na == 4:
-                for b0 in (0, 2):
-                    pending.append((a_codes[:, b0 * 128:(b0 + 2) * 128], a_scales[:, b0 * 128:(b0 + 2) * 128], i, j0, j1, b0, 2, False))
-            else:
-                pending.append((a_codes, a_scales, i, j0, j1, a0, na, i == njobs - 1))
+        regrouped = [0]
 
-        def regroup(eng, a):
-            src = f_raw[a // 4][:, (a % 4) * 1024:(a % 4 + 1) * 1024].rearrange("p (t c i) -> p c t i", t=4, i=4)
-            dst = f_grp[a // 4][:, (a % 4) * 1024:(a % 4 + 1) * 1024].rearrange("p (c i t) -> p c t i", t=4, i=4)
-            if eng == "s":
+        def regroup_next():
+            a = regrouped[0]
+            regrouped[0] += 1
+            cols = slice((a % 4) * 1024, (a % 4 + 1) * 1024)
+            src = f_raw[a // 4][:, cols].rearrange("p (t c i) -> p c t i", t=4, i=4)
+            dst = f_grouped[a // 4][:, cols].rearrange("p (c i t) -> p c t i", t=4, i=4)
+            if a % 2 == 0:
                 nc.scalar.copy(out=dst, in_=src)
             else:
                 nc.vector.tensor_copy(out=dst, in_=src)
 
-        for n in range(XBUFS):
+        pairs_quantised = [0]
+
+        def quantise_fwd_proj_pair():
+            k = pairs_quantised[0]
+            pairs_quantised[0] += 1
+            cols = slice(k * 512, (k + 1) * 512)
+            nc.vector.quantize_mx(out=f_codes[:, cols].bitcast(FP8X4), scales=f_scales[:, cols],
+                                  in_=f_grouped[k // 2][:, (k % 2) * 2048:(k % 2 + 1) * 2048])
+
+        for n in range(LOADS_AHEAD):
             load_next()
 
-        g = transpose_unit(0)
-        for r in range(2):
-            quantise_half(g, w_codes[0], w_scales[0], r)
-        g_job = transpose_unit(1)
-        codes = cpool.tile([128, 1024], U32, name="codes", tag="codes", align_bytes=64)
-        scales = cpool.tile([128, 1024], U8, name="scales", tag="scales", align_bytes=64)
-        for r in range(2):
-            quantise_half(g_job, codes, scales, r)
-        g = transpose_unit(2)
-        for r in range(2):
-            quantise_half(g, w_codes[1], w_scales[1], r)
+        codes_of = {0: new_codes()}
+        for n, (codes, scales) in enumerate([(w_codes[0], w_scales[0]), codes_of[0], (w_codes[1], w_scales[1])]):
+            transpose_strips(n, (0, 1, 2, 3))
+            for r in range(2):
+                quantise_half(n, codes, scales, r)
 
-        regrouped = [0]
-        fquant = [0]
         for i in range(njobs):
-            kind, j0, j1 = jobs[i]
-            nreg = NREG.get(i, 0)
-            nfq = NFQ.get(i, 0)
+            kind, j, half = jobs[i]
+            agg = None
             if kind == "edge":
-                agg = apool.tile([128, 2048], BF16, name="agg", tag="agg", align_bytes=64)
-            steps = STEPS_A if i < RSTART else STEPS_B if i < njobs - 2 else STEPS_C if i == njobs - 2 else STEPS_D
+                agg = agg_pool.tile([128, 2048], BF16, name="agg", tag="agg", align_bytes=64)
+            codes, scales = codes_of[i]
+            if i < last:
+                codes_of[i + 1] = new_codes()
+            run_before = {2: (0, 1), 3: (2, 3)} if i == 0 else {0: (0, 1), 2: (2, 3)}
+            for strip in range(4):
+                if i < last and strip in run_before:
+                    transpose_strips(i + 3, run_before[strip])
+                    if i == 0 and strip == 3:
+                        quantise_half(i + 3, *codes_of[i + 1], 0)
+                acc = project(0 if kind == "node" else 1, codes, scales, strip)
+                add_out(acc, i, strip, agg)
+                if i in REGROUP_JOBS and strip < 2:
+                    regroup_next()
+                if i < last and strip % 2 == 1 and (i > 0 or strip == 3):
+                    quantise_half(i + 3, *codes_of[i + 1], strip // 2)
+                if i in QUANTISE_JOBS and strip == 1:
+                    quantise_fwd_proj_pair()
+                if i > 0:
+                    sort_strip(i + SORT_AHEAD, strip)
+                if i == last and strip == 2:
+                    quantise_agg(agg, i, 0, 2)
+                if i == last and strip == 3:
+                    quantise_agg(agg, i, 2, 1)
+                    quantise_agg(agg, i, 3, 1)
+                if i >= FIRST_SECOND and strip != (0 if i == last else 3):
+                    second_product(i)
             if i == 0:
-                steps = "P0 A0 P1 A1 P2 A2 P3 A3 T q0 q1 x0 x1 x2 x3"
-            accs = {}
-            for step in steps.split(" "):
-                op = step[0]
-                aa = int(step[1]) if len(step) > 1 else 0
-                if op == "U" and i + 3 < len(srcs):
-                    transpose_unit(i + 3, (2, 3), g_next)
-                elif op in "TS" and i + 3 < len(srcs):
-                    g_next = transpose_unit(i + 3, (0, 1) if op == "S" else (0, 1, 2, 3))
-                    codes_next = cpool.tile([128, 1024], U32, name="codes", tag="codes", align_bytes=64)
-                    scales_next = cpool.tile([128, 1024], U8, name="scales", tag="scales", align_bytes=64)
-                elif op == "P":
-                    accs[aa] = project(0 if kind == "node" else 1, codes, scales, aa)
-                elif op == "A":
-                    acc_v = accs[aa][:].rearrange("p (t c i) -> p c t i", t=4, i=4)
-                    if kind == "node":
-                        j = j0 * 4 + aa
-                        nc.vector.tensor_tensor(out=nodeb[:, j * 512:(j + 1) * 512].rearrange("p (c t i) -> p c t i", t=4, i=4),
-                                                in0=acc_v, in1=bias32[:].unsqueeze(1).unsqueeze(3).to_broadcast([128, 32, 4, 4]), op=ADD)
-                    else:
-                        nc.vector.tensor_tensor(out=agg[:, aa * 512:(aa + 1) * 512].rearrange("p (c i t) -> p c t i", t=4, i=4),
-                                                in0=acc_v,
-                                                in1=nodeb[:, j0 * 512:(j0 + 1) * 512].rearrange("p (c t i) -> p c t i", t=4, i=4),
-                                                op=ADD)
-                    if nreg > 0:
-                        regroup(RENG[regrouped[0] % len(RENG)], regrouped[0])
-                        regrouped[0] += 1
-                        nreg -= 1
-                elif op == "G" and kind == "edge":
-                    quantise_agg(agg, i, 0, 4)
-                elif op == "q" and i + 3 < len(srcs):
-                    quantise_half(g_next, codes_next, scales_next, aa)
-                elif op == "x":
-                    presort(i + LOOK, aa)
-                elif op == "g" and kind == "edge":
-                    if i == njobs - 1:
-                        quantise_agg(agg, i, aa, 2 if aa == 0 else 1)
-                    else:
-                        quantise_agg(agg, i, aa * 2, 2)
-                elif op == "R" and i >= RSTART:
-                    rep_pair(i)
-                if op in "qQ" and nfq > 0:
-                    c0 = fquant[0] * 512
-                    nc.vector.quantize_mx(out=f_codes[:, c0:c0 + 512].bitcast(FP8X4),
-                                          scales=f_scales[:, c0:c0 + 512],
-                                          in_=f_grp[fquant[0] // 2][:, (fquant[0] % 2) * 2048:(fquant[0] % 2 + 1) * 2048])
-                    fquant[0] += 1
-                    nfq -= 1
-            if i + 1 < njobs:
-                codes, scales = codes_next, scales_next
-        for n in range(len(pending) - done[0]):
-            rep_pair(njobs)
+                for strip in range(4):
+                    sort_strip(i + SORT_AHEAD, strip)
+            if kind == "edge" and i < last:
+                quantise_agg(agg, i, 0, 4)
+        while waiting:
+            second_product(njobs)

from contextlib import ExitStack

import concourse.bass as bass
import concourse.mybir as mybir
import concourse.tile as tile
from concourse.masks import make_identity

F32 = mybir.dt.float32
BF16 = mybir.dt.bfloat16
U32 = mybir.dt.uint32
U8 = mybir.dt.uint8
FP8X4 = mybir.dt.float8_e4m3fn_x4
ADD = mybir.AluOpType.add

B, A, E, P, R = 1024, 8, 1024, 512, 256
FLOPS = 2 * (B * E * P + B * A * E * P + B * A * P * R)

LOADS_AHEAD = 6
SORT_AHEAD = 5
FIRST_SORTED = 5
FIRST_LATE = 15
FWD_PROJ_BEHIND = {6: 0, 7: 1}
REGROUP_JOBS = (3, 4, 5, 6)
QUANTISE_JOBS = (5, 6, 7, 8)
FIRST_SECOND = 8


def sorter(n, strip):
    if n < FIRST_SORTED:
        return None
    if n < FIRST_LATE:
        return ("scalar", None, "scalar", None)[strip]
    return ("vector", "vector", "scalar", None)[strip]


def tile_attributegnn_pa_t_kernel(tc, image_features, edge_attributes, linear_w, linear_b, fwd_proj, out):
    nc = tc.nc
    w_v = linear_w.rearrange("(q t) (h k) -> h q t k", t=4, h=2)
    image_v = image_features.rearrange("(c j) k -> c (j k)", j=8)
    edge_v = edge_attributes.rearrange("(c j) a k -> c j (a k)", j=8)
    f_v = fwd_proj.rearrange("a (q t) r -> q a (t r)", t=4)
    out_v = out.rearrange("(c j) a r -> c j (a r)", j=8)
    b_v = linear_b.rearrange("(q t) -> q t", t=4)

    with ExitStack() as ctx:
        const = ctx.enter_context(tc.tile_pool(name="const", bufs=1))
        load_pool = ctx.enter_context(tc.tile_pool(name="load_pool", bufs=LOADS_AHEAD))
        sort_pool = ctx.enter_context(tc.tile_pool(name="sort_pool", bufs=3))
        turn_pool = ctx.enter_context(tc.tile_pool(name="turn_pool", bufs=3))
        code_pool = ctx.enter_context(tc.tile_pool(name="code_pool", bufs=3))
        agg_pool = ctx.enter_context(tc.tile_pool(name="agg_pool", bufs=3))
        agg_code_pool = ctx.enter_context(tc.tile_pool(name="agg_code_pool", bufs=9))
        out_pool = ctx.enter_context(tc.tile_pool(name="out_pool", bufs=3))
        psum = ctx.enter_context(tc.psum_pool(name="psum", bufs=1))
        ctx.enter_context(tc.manual_schedule())

        banks_used = [0]

        def next_bank():
            k = banks_used[0] % 8
            banks_used[0] += 1
            return psum.tile([128, 512], F32, name="bank%d" % k, tag="bank%d" % k)

        ident = const.tile([128, 128], F32, name="ident")
        make_identity(nc, ident[:])
        bias_bf = const.tile([128, 4], BF16, name="bias_bf")
        with nc.allow_non_contiguous_dma(reason="512 bias values, four to a partition"):
            nc.scalar.dma_start(out=bias_bf[:], in_=b_v)
        bias32 = const.tile([128, 4], F32, name="bias32")
        nc.vector.tensor_copy(out=bias32[:], in_=bias_bf[:])
        node_sums = const.tile([128, 4096], F32, name="node_sums")
        w_codes = [const.tile([128, 1024], U32, name="w_codes%d" % h, align_bytes=64) for h in range(2)]
        w_scales = [const.tile([128, 1024], U8, name="w_scales%d" % h, align_bytes=64) for h in range(2)]
        f_codes = const.tile([128, 2048], U32, name="f_codes", align_bytes=64)
        f_scales = const.tile([128, 2048], U8, name="f_scales", align_bytes=64)
        f_raw = [const.tile([128, 4096], BF16, name="f_raw%d" % h) for h in range(2)]
        f_grouped = [const.tile([128, 4096], BF16, name="f_grouped%d" % h, align_bytes=64) for h in range(2)]

        jobs = []
        for quad in range(2):
            jobs.append(("node", quad, 0))
            jobs.extend([("edge", 4 * quad + u // 2, u % 2) for u in range(8)])
        njobs = len(jobs)
        last = njobs - 1

        sources = [("w", 0), ("job", 0), ("w", 1)] + [("job", i) for i in range(1, njobs)]
        loaded = []

        def load_next():
            n = len(loaded)
            if n >= len(sources):
                return
            kind, idx = sources[n]
            x = load_pool.tile([128, 4096], BF16, name="x", tag="x")
            if kind == "w":
                for t in range(4):
                    nc.sync.dma_start(out=x[:, t * 1024:(t + 1) * 1024], in_=w_v[idx][:, t, :])
            else:
                job_kind, j, half = jobs[idx]
                if idx == 0:
                    for t in range(4):
                        nc.sync.dma_start(out=x[:, t * 1024:(t + 1) * 1024], in_=image_v[:, t * 1024:(t + 1) * 1024])
                elif job_kind == "node":
                    nc.sync.dma_start(out=x[:], in_=image_v[:, j * 4096:(j + 1) * 4096])
                else:
                    nc.sync.dma_start(out=x[:], in_=edge_v[:, j, half * 4096:(half + 1) * 4096])
            loaded.append(x)
            if n in FWD_PROJ_BEHIND:
                h = FWD_PROJ_BEHIND[n]
                nc.sync.dma_start(out=f_raw[h][:].rearrange("p (a s) -> p a s", a=4), in_=f_v[:, h * 4:(h + 1) * 4, :])

        sorted_tiles = {}

        def sort_strip(n, strip):
            if n >= len(sources) or sorter(n, strip) is None:
                return
            if n not in sorted_tiles:
                sorted_tiles[n] = sort_pool.tile([128, 2048], F32, name="sorted_words", tag="sorted_words")
            cols = slice(strip * 512, (strip + 1) * 512)
            dst = sorted_tiles[n][:, cols].rearrange("p (g u c) -> p g u c", g=2, u=2)
            src = loaded[n][:].bitcast(F32)[:, cols].rearrange("p (g c u) -> p g u c", g=2, u=2)
            if sorter(n, strip) == "scalar":
                nc.scalar.copy(out=dst, in_=src)
            else:
                nc.vector.tensor_copy(out=dst, in_=src)

        turned = {}

        def transpose_strips(n, strips):
            if n not in turned:
                turned[n] = turn_pool.tile([128, 4096], BF16, name="turned", tag="turned", align_bytes=64)
            words = loaded[n][:].bitcast(F32)
            turned_words = turned[n][:].bitcast(F32).rearrange("p (r g a c u) -> p r g a c u", r=2, g=2, a=2, c=128, u=2)
            for strip in strips:
                bank = next_bank()
                for s in range(4):
                    g, u = s // 2, s % 2
                    if sorter(n, strip) is None:
                        col = strip * 512 + g * 256 + u
                        part = words[:, col:col + 255:2]
                    else:
                        col = strip * 512 + s * 128
                        part = sorted_tiles[n][:, col:col + 128]
                    nc.tensor.transpose(bank[:, s * 128:(s + 1) * 128], part, ident[:])
                nc.scalar.copy(out=turned_words[:, strip // 2, :, strip % 2, :, :],
                               in_=bank[:].rearrange("p (g u c) -> p g c u", g=2, u=2, c=128))
            if 3 in strips:
                load_next()

        def quantise_half(n, codes, scales, r):
            nc.vector.quantize_mx(out=codes[:, r * 512:(r + 1) * 512].bitcast(FP8X4),
                                  scales=scales[:, r * 512:(r + 1) * 512],
                                  in_=turned[n][:, r * 2048:(r + 1) * 2048])

        def new_codes():
            codes = code_pool.tile([128, 1024], U32, name="codes", tag="codes", align_bytes=64)
            scales = code_pool.tile([128, 1024], U8, name="scales", tag="scales", align_bytes=64)
            return codes, scales

        def project(h, codes, scales, strip):
            acc = next_bank()
            for t in range(4):
                for g in range(2):
                    wc = (t // 2) * 512 + g * 256 + (t % 2) * 128
                    dc = (strip // 2) * 512 + g * 256 + (strip % 2) * 128
                    nc.tensor.matmul_mx(out=acc[:, t * 128:(t + 1) * 128],
                                        lhsT=w_codes[h][:, wc:wc + 128].bitcast(FP8X4),
                                        lhsT_scale=w_scales[h][:, wc:wc + 128],
                                        rhs=codes[:, dc:dc + 128].bitcast(FP8X4),
                                        rhs_scale=scales[:, dc:dc + 128],
                                        start=(g == 0), stop=(g == 1))
            return acc

        def add_out(acc, i, strip, agg):
            kind, j, half = jobs[i]
            acc_v = acc[:].rearrange("p (t c i) -> p c t i", t=4, i=4)
            if kind == "node":
                j = j * 4 + strip
                nc.vector.tensor_tensor(out=node_sums[:, j * 512:(j + 1) * 512].rearrange("p (c t i) -> p c t i", t=4, i=4),
                                        in0=acc_v,
                                        in1=bias32[:].unsqueeze(1).unsqueeze(3).to_broadcast([128, 32, 4, 4]),
                                        op=ADD)
            else:
                nc.vector.tensor_tensor(out=agg[:, strip * 512:(strip + 1) * 512].rearrange("p (c i t) -> p c t i", t=4, i=4),
                                        in0=acc_v,
                                        in1=node_sums[:, j * 512:(j + 1) * 512].rearrange("p (c t i) -> p c t i", t=4, i=4),
                                        op=ADD)

        waiting = []
        out_tiles = {}

        def quantise_agg(agg, i, first, count):
            codes = agg_code_pool.tile([128, 512], U32, name="agg_codes", tag="agg_codes", align_bytes=64)
            scales = agg_code_pool.tile([128, 512], U8, name="agg_scales", tag="agg_scales", align_bytes=64)
            nc.vector.quantize_mx(out=codes[:, 0:count * 128].bitcast(FP8X4), scales=scales[:, 0:count * 128],
                                  in_=agg[:, first * 512:(first + count) * 512])
            for k in range(0, count, 2):
                pair = min(2, count - k)
                cols = slice(k * 128, (k + pair) * 128)
                waiting.append((codes[:, cols], scales[:, cols], i, first + k, pair))

        def second_product(before):
            if not waiting or waiting[0][2] >= before:
                return
            codes, scales, i, first, count = waiting.pop(0)
            kind, j, half = jobs[i]
            if first == 0:
                out_tiles[i] = out_pool.tile([128, 1024], F32, name="out_tile", tag="out_tile")
            o = out_tiles[i]
            bank = next_bank()
            for s in range(count):
                a = half * 4 + first + s
                nc.tensor.matmul_mx(out=bank[:, s * 256:(s + 1) * 256],
                                    lhsT=codes[:, s * 128:(s + 1) * 128].bitcast(FP8X4),
                                    lhsT_scale=scales[:, s * 128:(s + 1) * 128],
                                    rhs=f_codes[:, a * 256:(a + 1) * 256].bitcast(FP8X4),
                                    rhs_scale=f_scales[:, a * 256:(a + 1) * 256],
                                    start=True, stop=True)
            end = first + count
            nc.scalar.copy(out=o[:, first * 256:end * 256], in_=bank[:, 0:count * 256])
            if i == last:
                nc.sync.dma_start(out=out_v[:, j, half * 1024 + first * 256:half * 1024 + end * 256],
                                  in_=o[:, first * 256:end * 256])
            elif end == 4:
                nc.sync.dma_start(out=out_v[:, j, half * 1024:(half + 1) * 1024], in_=o[:])

        regrouped = [0]

        def regroup_next():
            a = regrouped[0]
            regrouped[0] += 1
            cols = slice((a % 4) * 1024, (a % 4 + 1) * 1024)
            src = f_raw[a // 4][:, cols].rearrange("p (t c i) -> p c t i", t=4, i=4)
            dst = f_grouped[a // 4][:, cols].rearrange("p (c i t) -> p c t i", t=4, i=4)
            if a % 2 == 0:
                nc.scalar.copy(out=dst, in_=src)
            else:
                nc.vector.tensor_copy(out=dst, in_=src)

        pairs_quantised = [0]

        def quantise_fwd_proj_pair():
            k = pairs_quantised[0]
            pairs_quantised[0] += 1
            cols = slice(k * 512, (k + 1) * 512)
            nc.vector.quantize_mx(out=f_codes[:, cols].bitcast(FP8X4), scales=f_scales[:, cols],
                                  in_=f_grouped[k // 2][:, (k % 2) * 2048:(k % 2 + 1) * 2048])

        for n in range(LOADS_AHEAD):
            load_next()

        codes_of = {0: new_codes()}
        for n, (codes, scales) in enumerate([(w_codes[0], w_scales[0]), codes_of[0], (w_codes[1], w_scales[1])]):
            transpose_strips(n, (0, 1, 2, 3))
            for r in range(2):
                quantise_half(n, codes, scales, r)

        for i in range(njobs):
            kind, j, half = jobs[i]
            agg = None
            if kind == "edge":
                agg = agg_pool.tile([128, 2048], BF16, name="agg", tag="agg", align_bytes=64)
            codes, scales = codes_of[i]
            if i < last:
                codes_of[i + 1] = new_codes()
            run_before = {2: (0, 1), 3: (2, 3)} if i == 0 else {0: (0, 1), 2: (2, 3)}
            for strip in range(4):
                if i < last and strip in run_before:
                    transpose_strips(i + 3, run_before[strip])
                    if i == 0 and strip == 3:
                        quantise_half(i + 3, *codes_of[i + 1], 0)
                acc = project(0 if kind == "node" else 1, codes, scales, strip)
                add_out(acc, i, strip, agg)
                if i in REGROUP_JOBS and strip < 2:
                    regroup_next()
                if i < last and strip % 2 == 1 and (i > 0 or strip == 3):
                    quantise_half(i + 3, *codes_of[i + 1], strip // 2)
                if i in QUANTISE_JOBS and strip == 1:
                    quantise_fwd_proj_pair()
                if i > 0:
                    sort_strip(i + SORT_AHEAD, strip)
                if i == last and strip == 2:
                    quantise_agg(agg, i, 0, 2)
                if i == last and strip == 3:
                    quantise_agg(agg, i, 2, 1)
                    quantise_agg(agg, i, 3, 1)
                if i >= FIRST_SECOND and strip != (0 if i == last else 3):
                    second_product(i)
            if i == 0:
                for strip in range(4):
                    sort_strip(i + SORT_AHEAD, strip)
            if kind == "edge" and i < last:
                quantise_agg(agg, i, 0, 4)
        while waiting:
            second_product(njobs)
